import numpy as np
import ml_dtypes


def mxq(x, axis, fmt="e4m3"):
    dtype, down = {"e4m3": (ml_dtypes.float8_e4m3fn, 7), "e5m2": (ml_dtypes.float8_e5m2, 14)}[fmt]
    v = np.moveaxis(np.asarray(x, np.float32).astype(ml_dtypes.bfloat16).astype(np.float64), axis, -1)
    blocks = v.reshape(v.shape[:-1] + (-1, 32))
    amax = np.abs(blocks).max(-1, keepdims=True)
    byte = np.maximum(np.where(amax > 0, np.frexp(amax)[1] - 1 + 127, 0) - down, 1)
    scale = np.exp2(byte - 127.0)
    codes = (blocks / scale).astype(np.float32).astype(dtype).astype(np.float64)
    return np.moveaxis((codes * scale).reshape(v.shape), -1, axis)


WIDE = False


def mx_kscale(k):
    if not WIDE:
        return np.ones(k)
    levels = np.array([30, -30])
    if k % 512:
        return np.exp2(np.random.permutation(np.resize(levels, k // 32))).repeat(32)
    a = np.empty((k // 512, 16))
    for p in range(k // 512):
        a[p, :8] = np.random.permutation(np.resize(levels, 8))
        for g in range(8):
            far = levels[np.abs(levels - a[p, g]) >= 10]
            a[p, g + 8] = far[np.random.randint(len(far))]
    return np.exp2(a.ravel()).repeat(32)


BF16 = ml_dtypes.bfloat16


def bf(x):
    return np.asarray(x, np.float32).astype(BF16)


def f64(x):
    return np.asarray(x).astype(np.float64)


B, S, HID, H, D = 1, 1024, 1024, 8, 128
QKV = 3 * H * D


def rotate_half(x):
    x1, x2 = x[..., : x.shape[-1] // 2], x[..., x.shape[-1] // 2 :]
    return np.concatenate((-x2, x1), axis=-1)


def setup_inputs():
    s = mx_kscale(HID)
    return {"hidden_states": bf(np.random.standard_normal((B, S, HID)) * s),
            "cos": bf(np.random.uniform(size=(S, D))),
            "sin": bf(np.random.uniform(size=(S, D))),
            "w_qkv": bf(np.random.standard_normal((HID, QKV)) * 2.0 / np.sqrt(HID) / s[:, None])}


def reference(hidden_states, cos, sin, w_qkv):
    qkv = mxq(f64(hidden_states), 2, "e5m2") @ mxq(f64(w_qkv), 0, "e5m2")
    qkv = qkv.reshape(B, S, 3 * H, D)
    q, k, v = qkv[:, :, :H], qkv[:, :, H:2 * H], qkv[:, :, 2 * H:]
    c = f64(cos)[:, None, :]
    sn = f64(sin)[:, None, :]
    q_rot = q * c + rotate_half(q) * sn
    k_rot = k * c + rotate_half(k) * sn
    return q_rot, k_rot, v

@@ -1,0 +1,257 @@
+from contextlib import ExitStack
+
+import concourse.mybir as mybir
+from concourse.masks import make_identity
+
+F32 = mybir.dt.float32
+BF16 = mybir.dt.bfloat16
+U32 = mybir.dt.uint32
+U8 = mybir.dt.uint8
+E5M2X4 = mybir.dt.float8_e5m2_x4
+MULT = mybir.AluOpType.mult
+ADD = mybir.AluOpType.add
+
+SEQ, HID, HEADS, DH = 1024, 1024, 8, 128
+QKV = 3 * HEADS * DH
+FLOPS = 2 * SEQ * HID * QKV
+
+P = 128
+PACK = 4
+K_PASS = P * PACK
+PASSES = HID // K_PASS
+N_TILE = 512
+HEADS_PER_BANK = N_TILE // DH
+HALF = DH // 2
+TOK_TILES = SEQ // P
+ROPE_CHUNKS = 4
+N_CHUNKS = QKV // N_TILE
+
+LOAD_ORDER = (
+    ("x", 0), ("w", 0, 0), ("w", 0, 1), ("sin",), ("cos",), ("x", 1), ("x", 2), ("x", 3), ("w", 1, 0),
+    ("x", 4), ("x", 5), ("w", 1, 1), ("x", 6), ("x", 7), ("w", 2, 0), ("w", 2, 1), ("w", 4, 0), ("w", 4, 1),
+)
+LOAD_WIDTH = {0: N_TILE, 1: N_TILE, 2: 2 * N_TILE, 4: 2 * N_TILE}
+CHUNK_ORDER = (1, 2, 4, 3, 5)
+QW_SLOT = {1: 6, 2: 10, 4: 14, 3: 18, 5: 22}
+V_START = {4: 15, 5: 23}
+VECTOR_ADDS = (10, 20, 30, 31)
+PIECE = 256
+
+
+def tile_attention_pa_kernel(tc, hidden_states, cos, sin, w_qkv, out_0, out_1, out_2):
+    nc = tc.nc
+    outs = (out_0, out_1, out_2)
+
+    with ExitStack() as ctx:
+        keep = ctx.enter_context(tc.tile_pool(name="keep", bufs=1))
+        wgrp_pool = ctx.enter_context(tc.tile_pool(name="wgrp_pool", bufs=3))
+        prod_pool = ctx.enter_context(tc.tile_pool(name="prod_pool", bufs=4))
+        res_pool = ctx.enter_context(tc.tile_pool(name="res_pool", bufs=10))
+        vres_pool = ctx.enter_context(tc.tile_pool(name="vres_pool", bufs=4))
+        rope_ps = ctx.enter_context(tc.psum_pool(name="rope_ps", bufs=5))
+        aux_ps = ctx.enter_context(tc.psum_pool(name="aux_ps", bufs=3))
+
+        ident = keep.tile([P, P], F32, name="ident")
+        make_identity(nc, ident[:])
+
+        pairs = TOK_TILES // 2
+        x_raw = [keep.tile([P, HID], BF16, name="x_raw%d" % m) for m in range(TOK_TILES)]
+        x_grp = [keep.tile([P, 2, PASSES, P, PACK], BF16, name="x_grp%d" % i, align_bytes=64) for i in range(pairs)]
+        x_codes = [keep.tile([P, 2, PASSES * P], U32, name="x_codes%d" % i, align_bytes=64) for i in range(pairs)]
+        x_scales = [keep.tile([P, 2, PASSES * P], U8, name="x_scales%d" % i, align_bytes=64) for i in range(pairs)]
+        w_raw = {}
+        for c in LOAD_WIDTH:
+            width = LOAD_WIDTH[c]
+            for g in range(PASSES):
+                raw = keep.tile([P, PACK, width], BF16, name="w_raw%d_%d" % (c, g))
+                for k in range(width // N_TILE):
+                    w_raw[(c + k, g)] = raw[:, :, k * N_TILE:(k + 1) * N_TILE]
+                w_raw[("load", c, g)] = raw
+        w_codes = [keep.tile([P, PASSES, N_TILE], U32, name="w_codes%d" % c, align_bytes=64) for c in range(N_CHUNKS)]
+        w_scales = [keep.tile([P, PASSES, N_TILE], U8, name="w_scales%d" % c, align_bytes=64) for c in range(N_CHUNKS)]
+        sin_sb = keep.tile([P, TOK_TILES, DH], BF16, name="sin_sb")
+        cos_sb = keep.tile([P, TOK_TILES, DH], BF16, name="cos_sb")
+        table = keep.tile([P, TOK_TILES, 4, HALF], BF16, name="table")
+        warm_in = keep.tile([P, 8], F32, name="warm_in")
+        warm_out = keep.tile([P, 8], F32, name="warm_out")
+        w_grp = {}
+        x_bank = {}
+
+        def load(item):
+            if item[0] == "x":
+                m = item[1]
+                nc.sync.dma_start(out=x_raw[m][:], in_=hidden_states[0, m * P:(m + 1) * P, :])
+            elif item[0] == "w":
+                c, g = item[1], item[2]
+                nc.sync.dma_start(
+                    out=w_raw[("load", c, g)][:],
+                    in_=w_qkv[g * K_PASS:(g + 1) * K_PASS, c * N_TILE:c * N_TILE + LOAD_WIDTH[c]].rearrange(
+                        "(p j) w -> p j w", j=PACK),
+                )
+            elif item[0] == "sin":
+                nc.sync.dma_start(out=sin_sb[:], in_=sin.rearrange("(m p) d -> p m d", p=P))
+            else:
+                nc.sync.dma_start(out=cos_sb[:], in_=cos.rearrange("(m p) d -> p m d", p=P))
+
+        def transpose_x(m):
+            bank = aux_ps.tile([P, N_TILE], F32, name="aux_bank")
+            x_bank[m] = bank
+            words = x_raw[m][:].bitcast(F32)
+            view = bank[:].rearrange("p (g u r) -> p g u r", g=PASSES, u=2)
+            for g in range(PASSES):
+                for u in range(2):
+                    nc.tensor.transpose(view[:, g, u, :], words[:, 256 * g + u:256 * (g + 1):2], ident[:])
+
+        def copy_x(m):
+            nc.scalar.copy(
+                out=x_grp[m // 2][:, m % 2, :, :, :].bitcast(F32),
+                in_=x_bank[m][:].rearrange("p (g u r) -> p g r u", g=PASSES, u=2),
+            )
+
+        def quant_x_one(m):
+            nc.vector.quantize_mx(
+                out=x_codes[m // 2][:, m % 2, :].bitcast(E5M2X4),
+                scales=x_scales[m // 2][:, m % 2, :],
+                in_=x_grp[m // 2][:, m % 2, :, :, :].rearrange("p g r t -> p (g r t)"),
+            )
+
+        def quant_x_pair(i):
+            nc.vector.quantize_mx(
+                out=x_codes[i][:].rearrange("p a n -> p (a n)").bitcast(E5M2X4),
+                scales=x_scales[i][:].rearrange("p a n -> p (a n)"),
+                in_=x_grp[i][:].rearrange("p a g r t -> p (a g r t)"),
+            )
+
+        def interleave_w(engine_copy, c, g, s, h0=0, h1=HEADS_PER_BANK):
+            if c not in w_grp:
+                grouped = wgrp_pool.tile([P, PASSES, N_TILE, PACK], BF16, name="w_grouped", align_bytes=64)
+                w_grp[c] = grouped
+            if c < ROPE_CHUNKS:
+                lo = s * PIECE + h0 * HALF
+                hi = s * PIECE + h1 * HALF
+                engine_copy(
+                    out=w_grp[c][:, g, lo:hi, :].rearrange("p (h i) j -> p h i j", i=HALF),
+                    in_=w_raw[(c, g)].rearrange("p j (h s i) -> p s h i j", s=2, i=HALF)[:, s, h0:h1, :, :],
+                )
+            else:
+                engine_copy(
+                    out=w_grp[c][:, g, s * PIECE:(s + 1) * PIECE, :],
+                    in_=w_raw[(c, g)][:, :, s * PIECE:(s + 1) * PIECE].rearrange("p j w -> p w j"),
+                )
+
+        def quant_w_pass(c, g):
+            nc.vector.quantize_mx(
+                out=w_codes[c][:, g, :].bitcast(E5M2X4),
+                scales=w_scales[c][:, g, :],
+                in_=w_grp[c][:, g, :, :].rearrange("p w j -> p (w j)"),
+            )
+
+        def quant_w(c):
+            nc.vector.quantize_mx(
+                out=w_codes[c][:].rearrange("p g w -> p (g w)").bitcast(E5M2X4),
+                scales=w_scales[c][:].rearrange("p g w -> p (g w)"),
+                in_=w_grp[c][:].rearrange("p g w j -> p (g w j)"),
+            )
+
+        def matmul_bank(pool, bank_name, c, m):
+            acc = pool.tile([P, N_TILE], F32, name=bank_name)
+            for g in range(PASSES):
+                cols = slice(g * P, (g + 1) * P)
+                nc.tensor.matmul_mx(
+                    out=acc[:],
+                    lhsT=x_codes[m // 2][:, m % 2, cols].bitcast(E5M2X4),
+                    lhsT_scale=x_scales[m // 2][:, m % 2, cols],
+                    rhs=w_codes[c][:, g, :].bitcast(E5M2X4),
+                    rhs_scale=w_scales[c][:, g, :],
+                    start=(g == 0),
+                    stop=(g == PASSES - 1),
+                )
+            return acc
+
+        def out_rows(c, m):
+            h0 = (c % 2) * HEADS_PER_BANK
+            return outs[c // 2][0, m * P:(m + 1) * P, h0:h0 + HEADS_PER_BANK, :]
+
+        def rope_products(m, acc):
+            shape = [P, 2, 2, HEADS_PER_BANK, HALF]
+            prod = prod_pool.tile(shape, F32, name="prod")
+            nc.vector.tensor_tensor(
+                out=prod[:],
+                in0=acc[:].rearrange("p (s h i) -> p s h i", s=2, i=HALF).unsqueeze(2).to_broadcast(shape),
+                in1=table[:, m, :, :].rearrange("p (s w) i -> p s w i", s=2).unsqueeze(3).to_broadcast(shape),
+                op=MULT,
+            )
+            return prod
+
+        def rope_sum_store(engine, c, m, prod):
+            res = res_pool.tile([P, HEADS_PER_BANK, DH], F32, name="res")
+            engine.tensor_tensor(
+                out=res[:].rearrange("p h (s i) -> p s h i", s=2),
+                in0=prod[:, 0, :, :, :],
+                in1=prod[:, 1, :, :, :],
+                op=ADD,
+            )
+            nc.sync.dma_start(out=out_rows(c, m), in_=res[:])
+
+        def copy_v_store(c, m, acc):
+            vres = vres_pool.tile([P, HEADS_PER_BANK, DH], F32, name="vres")
+            nc.scalar.copy(out=vres[:].rearrange("p h d -> p (h d)"), in_=acc[:])
+            nc.sync.dma_start(out=out_rows(c, m), in_=vres[:])
+
+        with tc.manual_schedule():
+            nc.vector.memset(warm_in[:], 0.0)
+            nc.scalar.copy(out=warm_out[:], in_=warm_in[:])
+            for item in LOAD_ORDER:
+                load(item)
+
+            nc.gpsimd.tensor_scalar(out=table[:, :, 1, :], in0=sin_sb[:, :, HALF:DH],
+                                    scalar1=1.0, scalar2=0.0, op0=MULT, op1=ADD)
+            nc.gpsimd.tensor_scalar(out=table[:, :, 2, :], in0=sin_sb[:, :, 0:HALF],
+                                    scalar1=-1.0, scalar2=0.0, op0=MULT, op1=ADD)
+
+            transpose_x(0)
+            copy_x(0)
+            interleave_w(nc.vector.tensor_copy, 0, 0, 0)
+            interleave_w(nc.scalar.copy, 0, 0, 1)
+            interleave_w(nc.vector.tensor_copy, 0, 1, 0)
+            interleave_w(nc.vector.tensor_copy, 0, 1, 1, 0, 2)
+            interleave_w(nc.scalar.copy, 0, 1, 1, 2, 4)
+            quant_x_one(0)
+            quant_w_pass(0, 0)
+            quant_w_pass(0, 1)
+            nc.scalar.copy(out=table[:, :, 0:4:3, :], in_=cos_sb[:].rearrange("p m (s i) -> p m s i", s=2))
+            transpose_x(1)
+            transpose_x(2)
+            copy_x(1)
+            copy_x(2)
+            quant_x_one(1)
+
+            pieces = [(c, g, h) for c in CHUNK_ORDER for g in range(PASSES) for h in range(N_TILE // PIECE)]
+            piece_slot = [i + (1 if i >= 1 else 0) for i in range(len(pieces))]
+            rope_jobs = [(c, m) for c in range(ROPE_CHUNKS) for m in range(TOK_TILES)]
+            for b, (c, m) in enumerate(rope_jobs):
+                new_pair = b % 2 == 0 and b + 3 < TOK_TILES
+                if new_pair and b > 0:
+                    transpose_x(b + 2)
+                    transpose_x(b + 3)
+                    copy_x(b + 2)
+                    copy_x(b + 3)
+                acc = matmul_bank(rope_ps, "rope_bank", c, m)
+                if b == 0:
+                    transpose_x(3)
+                    copy_x(3)
+                for i, (pc, pg, ph) in enumerate(pieces):
+                    if piece_slot[i] == b:
+                        interleave_w(nc.scalar.copy, pc, pg, ph)
+                for vc in (4, 5):
+                    vm = b - V_START[vc]
+                    if 0 <= vm < TOK_TILES:
+                        vacc = matmul_bank(aux_ps, "aux_bank", vc, vm)
+                        copy_v_store(vc, vm, vacc)
+                prod = rope_products(m, acc)
+                if new_pair:
+                    quant_x_pair(b // 2 + 1)
+                for qc in CHUNK_ORDER:
+                    if QW_SLOT[qc] == b:
+                        quant_w(qc)
+                rope_sum_store(nc.vector if b in VECTOR_ADDS else nc.gpsimd, c, m, prod)

@@ -27,15 +27,16 @@ ROPE_CHUNKS = 4
 N_CHUNKS = QKV // N_TILE
 
 LOAD_ORDER = (
-    ("x", 0), ("w", 0, 0), ("w", 0, 1), ("sin",), ("cos",), ("x", 1), ("x", 2), ("x", 3), ("w", 1, 0),
-    ("x", 4), ("x", 5), ("w", 1, 1), ("x", 6), ("x", 7), ("w", 2, 0), ("w", 2, 1), ("w", 4, 0), ("w", 4, 1),
+    ("x", 0), ("w", 0, 0), ("w", 0, 1), ("sin",), ("cos",), ("x", 1), ("x", 2), ("x", 3), ("x", 4), ("x", 5),
+    ("x", 6), ("x", 7), ("w", 1, 0), ("w", 1, 1), ("w", 2, 0), ("w", 2, 1), ("w", 4, 0), ("w", 4, 1),
 )
 LOAD_WIDTH = {0: N_TILE, 1: N_TILE, 2: 2 * N_TILE, 4: 2 * N_TILE}
-CHUNK_ORDER = (1, 2, 4, 3, 5)
-QW_SLOT = {1: 6, 2: 10, 4: 14, 3: 18, 5: 22}
-V_START = {4: 15, 5: 23}
-VECTOR_ADDS = (10, 20, 30, 31)
+CHUNK_ORDER = (1, 2, 3, 4, 5)
+QW_SLOT = {1: 6, 2: 10, 3: 14, 4: 17, 5: 21}
+V_START = {4: 18, 5: 23}
+VECTOR_ADDS = (30, 31)
 PIECE = 256
+FIRST_PIECE_SLOT = 3
 
 
 def tile_attention_pa_kernel(tc, hidden_states, cos, sin, w_qkv, out_0, out_1, out_2):
@@ -45,7 +46,7 @@ def tile_attention_pa_kernel(tc, hidden_states, cos, sin, w_qkv, out_0, out_1, o
     with ExitStack() as ctx:
         keep = ctx.enter_context(tc.tile_pool(name="keep", bufs=1))
         wgrp_pool = ctx.enter_context(tc.tile_pool(name="wgrp_pool", bufs=3))
-        prod_pool = ctx.enter_context(tc.tile_pool(name="prod_pool", bufs=4))
+        prod_pool = ctx.enter_context(tc.tile_pool(name="prod_pool", bufs=6))
         res_pool = ctx.enter_context(tc.tile_pool(name="res_pool", bufs=10))
         vres_pool = ctx.enter_context(tc.tile_pool(name="vres_pool", bufs=4))
         rope_ps = ctx.enter_context(tc.psum_pool(name="rope_ps", bufs=5))
@@ -54,11 +55,10 @@ def tile_attention_pa_kernel(tc, hidden_states, cos, sin, w_qkv, out_0, out_1, o
         ident = keep.tile([P, P], F32, name="ident")
         make_identity(nc, ident[:])
 
-        pairs = TOK_TILES // 2
         x_raw = [keep.tile([P, HID], BF16, name="x_raw%d" % m) for m in range(TOK_TILES)]
-        x_grp = [keep.tile([P, 2, PASSES, P, PACK], BF16, name="x_grp%d" % i, align_bytes=64) for i in range(pairs)]
-        x_codes = [keep.tile([P, 2, PASSES * P], U32, name="x_codes%d" % i, align_bytes=64) for i in range(pairs)]
-        x_scales = [keep.tile([P, 2, PASSES * P], U8, name="x_scales%d" % i, align_bytes=64) for i in range(pairs)]
+        x_grp = keep.tile([P, TOK_TILES, PASSES, P, PACK], BF16, name="x_grp", align_bytes=64)
+        x_codes = keep.tile([P, TOK_TILES, PASSES * P], U32, name="x_codes", align_bytes=64)
+        x_scales = keep.tile([P, TOK_TILES, PASSES * P], U8, name="x_scales", align_bytes=64)
         w_raw = {}
         for c in LOAD_WIDTH:
             width = LOAD_WIDTH[c]
@@ -104,22 +104,15 @@ def tile_attention_pa_kernel(tc, hidden_states, cos, sin, w_qkv, out_0, out_1, o
 
         def copy_x(m):
             nc.scalar.copy(
-                out=x_grp[m // 2][:, m % 2, :, :, :].bitcast(F32),
+                out=x_grp[:, m, :, :, :].bitcast(F32),
                 in_=x_bank[m][:].rearrange("p (g u r) -> p g r u", g=PASSES, u=2),
             )
 
-        def quant_x_one(m):
+        def quant_x(m0, m1):
             nc.vector.quantize_mx(
-                out=x_codes[m // 2][:, m % 2, :].bitcast(E5M2X4),
-                scales=x_scales[m // 2][:, m % 2, :],
-                in_=x_grp[m // 2][:, m % 2, :, :, :].rearrange("p g r t -> p (g r t)"),
-            )
-
-        def quant_x_pair(i):
-            nc.vector.quantize_mx(
-                out=x_codes[i][:].rearrange("p a n -> p (a n)").bitcast(E5M2X4),
-                scales=x_scales[i][:].rearrange("p a n -> p (a n)"),
-                in_=x_grp[i][:].rearrange("p a g r t -> p (a g r t)"),
+                out=x_codes[:, m0:m1, :].rearrange("p a n -> p (a n)").bitcast(E5M2X4),
+                scales=x_scales[:, m0:m1, :].rearrange("p a n -> p (a n)"),
+                in_=x_grp[:, m0:m1, :, :, :].rearrange("p a g r t -> p (a g r t)"),
             )
 
         def interleave_w(engine_copy, c, g, s, h0=0, h1=HEADS_PER_BANK):
@@ -159,8 +152,8 @@ def tile_attention_pa_kernel(tc, hidden_states, cos, sin, w_qkv, out_0, out_1, o
                 cols = slice(g * P, (g + 1) * P)
                 nc.tensor.matmul_mx(
                     out=acc[:],
-                    lhsT=x_codes[m // 2][:, m % 2, cols].bitcast(E5M2X4),
-                    lhsT_scale=x_scales[m // 2][:, m % 2, cols],
+                    lhsT=x_codes[:, m, cols].bitcast(E5M2X4),
+                    lhsT_scale=x_scales[:, m, cols],
                     rhs=w_codes[c][:, g, :].bitcast(E5M2X4),
                     rhs_scale=w_scales[c][:, g, :],
                     start=(g == 0),
@@ -216,7 +209,7 @@ def tile_attention_pa_kernel(tc, hidden_states, cos, sin, w_qkv, out_0, out_1, o
             interleave_w(nc.vector.tensor_copy, 0, 1, 0)
             interleave_w(nc.vector.tensor_copy, 0, 1, 1, 0, 2)
             interleave_w(nc.scalar.copy, 0, 1, 1, 2, 4)
-            quant_x_one(0)
+            quant_x(0, 1)
             quant_w_pass(0, 0)
             quant_w_pass(0, 1)
             nc.scalar.copy(out=table[:, :, 0:4:3, :], in_=cos_sb[:].rearrange("p m (s i) -> p m s i", s=2))
@@ -224,24 +217,23 @@ def tile_attention_pa_kernel(tc, hidden_states, cos, sin, w_qkv, out_0, out_1, o
             transpose_x(2)
             copy_x(1)
             copy_x(2)
-            quant_x_one(1)
+            quant_x(1, 2)
 
             pieces = [(c, g, h) for c in CHUNK_ORDER for g in range(PASSES) for h in range(N_TILE // PIECE)]
-            piece_slot = [i + (1 if i >= 1 else 0) for i in range(len(pieces))]
             rope_jobs = [(c, m) for c in range(ROPE_CHUNKS) for m in range(TOK_TILES)]
+            late = []
             for b, (c, m) in enumerate(rope_jobs):
-                new_pair = b % 2 == 0 and b + 3 < TOK_TILES
-                if new_pair and b > 0:
-                    transpose_x(b + 2)
-                    transpose_x(b + 3)
-                    copy_x(b + 2)
-                    copy_x(b + 3)
+                if b in (1, 2):
+                    for t in (2 * b + 2, 2 * b + 3):
+                        transpose_x(t)
+                    for t in (2 * b + 2, 2 * b + 3):
+                        copy_x(t)
                 acc = matmul_bank(rope_ps, "rope_bank", c, m)
                 if b == 0:
                     transpose_x(3)
                     copy_x(3)
                 for i, (pc, pg, ph) in enumerate(pieces):
-                    if piece_slot[i] == b:
+                    if FIRST_PIECE_SLOT + (3 * i) // 4 == b:
                         interleave_w(nc.scalar.copy, pc, pg, ph)
                 for vc in (4, 5):
                     vm = b - V_START[vc]
@@ -249,9 +241,16 @@ def tile_attention_pa_kernel(tc, hidden_states, cos, sin, w_qkv, out_0, out_1, o
                         vacc = matmul_bank(aux_ps, "aux_bank", vc, vm)
                         copy_v_store(vc, vm, vacc)
                 prod = rope_products(m, acc)
-                if new_pair:
-                    quant_x_pair(b // 2 + 1)
+                if b == 0:
+                    quant_x(2, 4)
+                if b == 2:
+                    quant_x(4, 8)
                 for qc in CHUNK_ORDER:
                     if QW_SLOT[qc] == b:
                         quant_w(qc)
-                rope_sum_store(nc.vector if b in VECTOR_ADDS else nc.gpsimd, c, m, prod)
+                if b in VECTOR_ADDS:
+                    late.append((c, m, prod))
+                else:
+                    rope_sum_store(nc.gpsimd, c, m, prod)
+            for c, m, prod in late:
+                rope_sum_store(nc.vector, c, m, prod)

@@ -32,9 +32,9 @@ LOAD_ORDER = (
 )
 LOAD_WIDTH = {0: N_TILE, 1: N_TILE, 2: 2 * N_TILE, 4: 2 * N_TILE}
 CHUNK_ORDER = (1, 2, 3, 4, 5)
-QW_SLOT = {1: 6, 2: 10, 3: 14, 4: 17, 5: 21}
+QW_SLOT = {1: 5, 2: 11, 3: 15, 4: 17, 5: 21}
 V_START = {4: 18, 5: 23}
-VECTOR_ADDS = (30, 31)
+VECTOR_PAIRS = (30,)
 PIECE = 256
 FIRST_PIECE_SLOT = 3
 
@@ -46,8 +46,8 @@ def tile_attention_pa_kernel(tc, hidden_states, cos, sin, w_qkv, out_0, out_1, o
     with ExitStack() as ctx:
         keep = ctx.enter_context(tc.tile_pool(name="keep", bufs=1))
         wgrp_pool = ctx.enter_context(tc.tile_pool(name="wgrp_pool", bufs=3))
-        prod_pool = ctx.enter_context(tc.tile_pool(name="prod_pool", bufs=6))
-        res_pool = ctx.enter_context(tc.tile_pool(name="res_pool", bufs=10))
+        prod_pool = ctx.enter_context(tc.tile_pool(name="prod_pool", bufs=3))
+        res_pool = ctx.enter_context(tc.tile_pool(name="res_pool", bufs=5))
         vres_pool = ctx.enter_context(tc.tile_pool(name="vres_pool", bufs=4))
         rope_ps = ctx.enter_context(tc.psum_pool(name="rope_ps", bufs=5))
         aux_ps = ctx.enter_context(tc.psum_pool(name="aux_ps", bufs=3))
@@ -165,26 +165,28 @@ def tile_attention_pa_kernel(tc, hidden_states, cos, sin, w_qkv, out_0, out_1, o
             h0 = (c % 2) * HEADS_PER_BANK
             return outs[c // 2][0, m * P:(m + 1) * P, h0:h0 + HEADS_PER_BANK, :]
 
-        def rope_products(m, acc):
+        def rope_products(m, acc, prod_half):
             shape = [P, 2, 2, HEADS_PER_BANK, HALF]
-            prod = prod_pool.tile(shape, F32, name="prod")
             nc.vector.tensor_tensor(
-                out=prod[:],
+                out=prod_half,
                 in0=acc[:].rearrange("p (s h i) -> p s h i", s=2, i=HALF).unsqueeze(2).to_broadcast(shape),
                 in1=table[:, m, :, :].rearrange("p (s w) i -> p s w i", s=2).unsqueeze(3).to_broadcast(shape),
                 op=MULT,
             )
-            return prod
 
         def rope_sum_store(engine, c, m, prod):
-            res = res_pool.tile([P, HEADS_PER_BANK, DH], F32, name="res")
+            res = res_pool.tile([P, 2, HEADS_PER_BANK, DH], F32, name="res")
             engine.tensor_tensor(
-                out=res[:].rearrange("p h (s i) -> p s h i", s=2),
-                in0=prod[:, 0, :, :, :],
-                in1=prod[:, 1, :, :, :],
+                out=res[:].rearrange("p b h (s i) -> p s b h i", s=2),
+                in0=prod[:, :, 0, :, :, :].rearrange("p b w h i -> p w b h i"),
+                in1=prod[:, :, 1, :, :, :].rearrange("p b w h i -> p w b h i"),
                 op=ADD,
             )
-            nc.sync.dma_start(out=out_rows(c, m), in_=res[:])
+            h0 = (c % 2) * HEADS_PER_BANK
+            nc.sync.dma_start(
+                out=outs[c // 2][0, m * P:(m + 2) * P, h0:h0 + HEADS_PER_BANK, :].rearrange("(b p) h d -> p b h d", p=P),
+                in_=res[:],
+            )
 
         def copy_v_store(c, m, acc):
             vres = vres_pool.tile([P, HEADS_PER_BANK, DH], F32, name="vres")
@@ -197,11 +199,6 @@ def tile_attention_pa_kernel(tc, hidden_states, cos, sin, w_qkv, out_0, out_1, o
             for item in LOAD_ORDER:
                 load(item)
 
-            nc.gpsimd.tensor_scalar(out=table[:, :, 1, :], in0=sin_sb[:, :, HALF:DH],
-                                    scalar1=1.0, scalar2=0.0, op0=MULT, op1=ADD)
-            nc.gpsimd.tensor_scalar(out=table[:, :, 2, :], in0=sin_sb[:, :, 0:HALF],
-                                    scalar1=-1.0, scalar2=0.0, op0=MULT, op1=ADD)
-
             transpose_x(0)
             copy_x(0)
             interleave_w(nc.vector.tensor_copy, 0, 0, 0)
@@ -212,6 +209,8 @@ def tile_attention_pa_kernel(tc, hidden_states, cos, sin, w_qkv, out_0, out_1, o
             quant_x(0, 1)
             quant_w_pass(0, 0)
             quant_w_pass(0, 1)
+            nc.scalar.copy(out=table[:, :, 1, :], in_=sin_sb[:, :, HALF:DH])
+            nc.scalar.mul(out=table[:, :, 2, :], in_=sin_sb[:, :, 0:HALF], mul=-1.0)
             nc.scalar.copy(out=table[:, :, 0:4:3, :], in_=cos_sb[:].rearrange("p m (s i) -> p m s i", s=2))
             transpose_x(1)
             transpose_x(2)
@@ -221,7 +220,7 @@ def tile_attention_pa_kernel(tc, hidden_states, cos, sin, w_qkv, out_0, out_1, o
 
             pieces = [(c, g, h) for c in CHUNK_ORDER for g in range(PASSES) for h in range(N_TILE // PIECE)]
             rope_jobs = [(c, m) for c in range(ROPE_CHUNKS) for m in range(TOK_TILES)]
-            late = []
+            prod = None
             for b, (c, m) in enumerate(rope_jobs):
                 if b in (1, 2):
                     for t in (2 * b + 2, 2 * b + 3):
@@ -240,17 +239,15 @@ def tile_attention_pa_kernel(tc, hidden_states, cos, sin, w_qkv, out_0, out_1, o
                     if 0 <= vm < TOK_TILES:
                         vacc = matmul_bank(aux_ps, "aux_bank", vc, vm)
                         copy_v_store(vc, vm, vacc)
-                prod = rope_products(m, acc)
+                if b % 2 == 0:
+                    prod = prod_pool.tile([P, 2, 2, 2, HEADS_PER_BANK, HALF], F32, name="prod")
+                rope_products(m, acc, prod[:, b % 2, :, :, :, :])
                 if b == 0:
                     quant_x(2, 4)
-                if b == 2:
+                if b == 3:
                     quant_x(4, 8)
                 for qc in CHUNK_ORDER:
                     if QW_SLOT[qc] == b:
                         quant_w(qc)
-                if b in VECTOR_ADDS:
-                    late.append((c, m, prod))
-                else:
-                    rope_sum_store(nc.gpsimd, c, m, prod)
-            for c, m, prod in late:
-                rope_sum_store(nc.vector, c, m, prod)
+                if b % 2 == 1:
+                    rope_sum_store(nc.vector if b - 1 in VECTOR_PAIRS else nc.gpsimd, c, m - 1, prod)

@@ -28,12 +28,12 @@ N_CHUNKS = QKV // N_TILE
 
 LOAD_ORDER = (
     ("x", 0), ("w", 0, 0), ("w", 0, 1), ("sin",), ("cos",), ("x", 1), ("x", 2), ("x", 3), ("x", 4), ("x", 5),
-    ("x", 6), ("x", 7), ("w", 1, 0), ("w", 1, 1), ("w", 2, 0), ("w", 2, 1), ("w", 4, 0), ("w", 4, 1),
+    ("x", 6), ("x", 7), ("w", 1, 0), ("w", 1, 1), ("w", 4, 0), ("w", 4, 1), ("w", 2, 0), ("w", 2, 1),
 )
 LOAD_WIDTH = {0: N_TILE, 1: N_TILE, 2: 2 * N_TILE, 4: 2 * N_TILE}
-CHUNK_ORDER = (1, 2, 3, 4, 5)
-QW_SLOT = {1: 5, 2: 11, 3: 15, 4: 17, 5: 21}
-V_START = {4: 18, 5: 23}
+CHUNK_ORDER = (1, 4, 2, 5, 3)
+QW_SLOT = {1: 5, 4: 9, 2: 13, 5: 19, 3: 21}
+V_START = {4: 10, 5: 20}
 VECTOR_PAIRS = (30,)
 PIECE = 256
 FIRST_PIECE_SLOT = 3
@@ -41,7 +41,8 @@ FIRST_PIECE_SLOT = 3
 
 def tile_attention_pa_kernel(tc, hidden_states, cos, sin, w_qkv, out_0, out_1, out_2):
     nc = tc.nc
-    outs = (out_0, out_1, out_2)
+    x_rows = hidden_states[0, :, :].rearrange("(p m) k -> p m k", p=P)
+    outs = [o[0, :, :, :].rearrange("(p m) h d -> p m h d", p=P) for o in (out_0, out_1, out_2)]
 
     with ExitStack() as ctx:
         keep = ctx.enter_context(tc.tile_pool(name="keep", bufs=1))
@@ -80,7 +81,7 @@ def tile_attention_pa_kernel(tc, hidden_states, cos, sin, w_qkv, out_0, out_1, o
         def load(item):
             if item[0] == "x":
                 m = item[1]
-                nc.sync.dma_start(out=x_raw[m][:], in_=hidden_states[0, m * P:(m + 1) * P, :])
+                nc.sync.dma_start(out=x_raw[m][:], in_=x_rows[:, m, :])
             elif item[0] == "w":
                 c, g = item[1], item[2]
                 nc.sync.dma_start(
@@ -89,9 +90,9 @@ def tile_attention_pa_kernel(tc, hidden_states, cos, sin, w_qkv, out_0, out_1, o
                         "(p j) w -> p j w", j=PACK),
                 )
             elif item[0] == "sin":
-                nc.sync.dma_start(out=sin_sb[:], in_=sin.rearrange("(m p) d -> p m d", p=P))
+                nc.sync.dma_start(out=sin_sb[:], in_=sin.rearrange("(p m) d -> p m d", p=P))
             else:
-                nc.sync.dma_start(out=cos_sb[:], in_=cos.rearrange("(m p) d -> p m d", p=P))
+                nc.sync.dma_start(out=cos_sb[:], in_=cos.rearrange("(p m) d -> p m d", p=P))
 
         def transpose_x(m):
             bank = aux_ps.tile([P, N_TILE], F32, name="aux_bank")
@@ -163,7 +164,7 @@ def tile_attention_pa_kernel(tc, hidden_states, cos, sin, w_qkv, out_0, out_1, o
 
         def out_rows(c, m):
             h0 = (c % 2) * HEADS_PER_BANK
-            return outs[c // 2][0, m * P:(m + 1) * P, h0:h0 + HEADS_PER_BANK, :]
+            return outs[c // 2][:, m, h0:h0 + HEADS_PER_BANK, :]
 
         def rope_products(m, acc, prod_half):
             shape = [P, 2, 2, HEADS_PER_BANK, HALF]
@@ -183,10 +184,7 @@ def tile_attention_pa_kernel(tc, hidden_states, cos, sin, w_qkv, out_0, out_1, o
                 op=ADD,
             )
             h0 = (c % 2) * HEADS_PER_BANK
-            nc.sync.dma_start(
-                out=outs[c // 2][0, m * P:(m + 2) * P, h0:h0 + HEADS_PER_BANK, :].rearrange("(b p) h d -> p b h d", p=P),
-                in_=res[:],
-            )
+            nc.sync.dma_start(out=outs[c // 2][:, m:m + 2, h0:h0 + HEADS_PER_BANK, :], in_=res[:])
 
         def copy_v_store(c, m, acc):
             vres = vres_pool.tile([P, HEADS_PER_BANK, DH], F32, name="vres")

@@ -193,7 +193,7 @@ def tile_attention_pa_kernel(tc, hidden_states, cos, sin, w_qkv, out_0, out_1, o
 
         with tc.manual_schedule():
             nc.vector.memset(warm_in[:], 0.0)
-            nc.scalar.copy(out=warm_out[:], in_=warm_in[:])
+            nc.scalar.mul(out=warm_out[:], in_=warm_in[:], mul=-1.0)
             for item in LOAD_ORDER:
                 load(item)
 

@@ -34,7 +34,9 @@ LOAD_WIDTH = {0: N_TILE, 1: N_TILE, 2: 2 * N_TILE, 4: 2 * N_TILE}
 CHUNK_ORDER = (1, 4, 2, 5, 3)
 QW_SLOT = {1: 5, 4: 9, 2: 13, 5: 19, 3: 21}
 V_START = {4: 10, 5: 20}
-VECTOR_PAIRS = (30,)
+GROUP_SIZES = (2,) * 16
+VECTOR_GROUPS = (15,)
+PROD_BUFS = 6
 PIECE = 256
 FIRST_PIECE_SLOT = 3
 
@@ -47,8 +49,7 @@ def tile_attention_pa_kernel(tc, hidden_states, cos, sin, w_qkv, out_0, out_1, o
     with ExitStack() as ctx:
         keep = ctx.enter_context(tc.tile_pool(name="keep", bufs=1))
         wgrp_pool = ctx.enter_context(tc.tile_pool(name="wgrp_pool", bufs=3))
-        prod_pool = ctx.enter_context(tc.tile_pool(name="prod_pool", bufs=3))
-        res_pool = ctx.enter_context(tc.tile_pool(name="res_pool", bufs=5))
+        prod_pool = ctx.enter_context(tc.tile_pool(name="prod_pool", bufs=PROD_BUFS))
         vres_pool = ctx.enter_context(tc.tile_pool(name="vres_pool", bufs=4))
         rope_ps = ctx.enter_context(tc.psum_pool(name="rope_ps", bufs=5))
         aux_ps = ctx.enter_context(tc.psum_pool(name="aux_ps", bufs=3))
@@ -166,25 +167,24 @@ def tile_attention_pa_kernel(tc, hidden_states, cos, sin, w_qkv, out_0, out_1, o
             h0 = (c % 2) * HEADS_PER_BANK
             return outs[c // 2][:, m, h0:h0 + HEADS_PER_BANK, :]
 
-        def rope_products(m, acc, prod_half):
-            shape = [P, 2, 2, HEADS_PER_BANK, HALF]
+        def rope_products(m, acc, prod_bank):
+            shape = [P, 2, HEADS_PER_BANK, 2, HALF]
             nc.vector.tensor_tensor(
-                out=prod_half,
-                in0=acc[:].rearrange("p (s h i) -> p s h i", s=2, i=HALF).unsqueeze(2).to_broadcast(shape),
-                in1=table[:, m, :, :].rearrange("p (s w) i -> p s w i", s=2).unsqueeze(3).to_broadcast(shape),
+                out=prod_bank,
+                in0=acc[:].rearrange("p (s h i) -> p s h i", s=2, i=HALF).unsqueeze(3).to_broadcast(shape),
+                in1=table[:, m, :, :].rearrange("p (s w) i -> p s w i", s=2).unsqueeze(2).to_broadcast(shape),
                 op=MULT,
             )
 
-        def rope_sum_store(engine, c, m, prod):
-            res = res_pool.tile([P, 2, HEADS_PER_BANK, DH], F32, name="res")
-            engine.tensor_tensor(
-                out=res[:].rearrange("p b h (s i) -> p s b h i", s=2),
-                in0=prod[:, :, 0, :, :, :].rearrange("p b w h i -> p w b h i"),
-                in1=prod[:, :, 1, :, :, :].rearrange("p b w h i -> p w b h i"),
-                op=ADD,
-            )
+        def rope_sum_store(engine, c, m, size, prod):
+            first = prod[:, :, 0, :, :, :].rearrange("p b h w i -> p b (h w i)")
+            second = prod[:, :, 1, :, :, :].rearrange("p b h w i -> p b (h w i)")
+            engine.tensor_tensor(out=first, in0=first, in1=second, op=ADD)
             h0 = (c % 2) * HEADS_PER_BANK
-            nc.sync.dma_start(out=outs[c // 2][:, m:m + 2, h0:h0 + HEADS_PER_BANK, :], in_=res[:])
+            nc.sync.dma_start(
+                out=outs[c // 2][:, m:m + size, h0:h0 + HEADS_PER_BANK, :],
+                in_=prod[:, :, 0, :, :, :].rearrange("p b h w i -> p b h (w i)"),
+            )
 
         def copy_v_store(c, m, acc):
             vres = vres_pool.tile([P, HEADS_PER_BANK, DH], F32, name="vres")
@@ -218,8 +218,11 @@ def tile_attention_pa_kernel(tc, hidden_states, cos, sin, w_qkv, out_0, out_1, o
 
             pieces = [(c, g, h) for c in CHUNK_ORDER for g in range(PASSES) for h in range(N_TILE // PIECE)]
             rope_jobs = [(c, m) for c in range(ROPE_CHUNKS) for m in range(TOK_TILES)]
+            group_of = [(g, k) for g, size in enumerate(GROUP_SIZES) for k in range(size)]
             prod = None
             for b, (c, m) in enumerate(rope_jobs):
+                group, place = group_of[b]
+                size = GROUP_SIZES[group]
                 if b in (1, 2):
                     for t in (2 * b + 2, 2 * b + 3):
                         transpose_x(t)
@@ -237,9 +240,9 @@ def tile_attention_pa_kernel(tc, hidden_states, cos, sin, w_qkv, out_0, out_1, o
                     if 0 <= vm < TOK_TILES:
                         vacc = matmul_bank(aux_ps, "aux_bank", vc, vm)
                         copy_v_store(vc, vm, vacc)
-                if b % 2 == 0:
-                    prod = prod_pool.tile([P, 2, 2, 2, HEADS_PER_BANK, HALF], F32, name="prod")
-                rope_products(m, acc, prod[:, b % 2, :, :, :, :])
+                if place == 0:
+                    prod = prod_pool.tile([P, size, 2, HEADS_PER_BANK, 2, HALF], F32, name="prod")
+                rope_products(m, acc, prod[:, place, :, :, :, :])
                 if b == 0:
                     quant_x(2, 4)
                 if b == 3:
@@ -247,5 +250,5 @@ def tile_attention_pa_kernel(tc, hidden_states, cos, sin, w_qkv, out_0, out_1, o
                 for qc in CHUNK_ORDER:
                     if QW_SLOT[qc] == b:
                         quant_w(qc)
-                if b % 2 == 1:
-                    rope_sum_store(nc.vector if b - 1 in VECTOR_PAIRS else nc.gpsimd, c, m - 1, prod)
+                if place == size - 1:
+                    rope_sum_store(nc.vector if group in VECTOR_GROUPS else nc.gpsimd, c, m - place, size, prod)

@@ -121,18 +121,12 @@ def tile_attention_pa_kernel(tc, hidden_states, cos, sin, w_qkv, out_0, out_1, o
             if c not in w_grp:
                 grouped = wgrp_pool.tile([P, PASSES, N_TILE, PACK], BF16, name="w_grouped", align_bytes=64)
                 w_grp[c] = grouped
-            if c < ROPE_CHUNKS:
-                lo = s * PIECE + h0 * HALF
-                hi = s * PIECE + h1 * HALF
-                engine_copy(
-                    out=w_grp[c][:, g, lo:hi, :].rearrange("p (h i) j -> p h i j", i=HALF),
-                    in_=w_raw[(c, g)].rearrange("p j (h s i) -> p s h i j", s=2, i=HALF)[:, s, h0:h1, :, :],
-                )
-            else:
-                engine_copy(
-                    out=w_grp[c][:, g, s * PIECE:(s + 1) * PIECE, :],
-                    in_=w_raw[(c, g)][:, :, s * PIECE:(s + 1) * PIECE].rearrange("p j w -> p w j"),
-                )
+            lo = s * PIECE + h0 * HALF
+            hi = s * PIECE + h1 * HALF
+            engine_copy(
+                out=w_grp[c][:, g, lo:hi, :].rearrange("p (u i) j -> p u j i", i=PACK),
+                in_=w_raw[(c, g)][:, :, lo:hi].rearrange("p j (u i) -> p u j i", i=PACK),
+            )
 
         def quant_w_pass(c, g):
             nc.vector.quantize_mx(
@@ -168,11 +162,11 @@ def tile_attention_pa_kernel(tc, hidden_states, cos, sin, w_qkv, out_0, out_1, o
             return outs[c // 2][:, m, h0:h0 + HEADS_PER_BANK, :]
 
         def rope_products(m, acc, prod_bank):
-            shape = [P, 2, HEADS_PER_BANK, 2, HALF]
+            shape = [P, HEADS_PER_BANK, 2, 2, HALF]
             nc.vector.tensor_tensor(
-                out=prod_bank,
-                in0=acc[:].rearrange("p (s h i) -> p s h i", s=2, i=HALF).unsqueeze(3).to_broadcast(shape),
-                in1=table[:, m, :, :].rearrange("p (s w) i -> p s w i", s=2).unsqueeze(2).to_broadcast(shape),
+                out=prod_bank.rearrange("p s h w i -> p h s w i"),
+                in0=acc[:].rearrange("p (h s i) -> p h s i", s=2, i=HALF).unsqueeze(3).to_broadcast(shape),
+                in1=table[:, m, :, :].rearrange("p (s w) i -> p s w i", s=2).unsqueeze(1).to_broadcast(shape),
                 op=MULT,
             )
 

@@ -34,8 +34,8 @@ LOAD_WIDTH = {0: N_TILE, 1: N_TILE, 2: 2 * N_TILE, 4: 2 * N_TILE}
 CHUNK_ORDER = (1, 4, 2, 5, 3)
 QW_SLOT = {1: 5, 4: 9, 2: 13, 5: 19, 3: 21}
 V_START = {4: 10, 5: 20}
-GROUP_SIZES = (2,) * 16
-VECTOR_GROUPS = (15,)
+GROUP_SIZES = (2,) * 15 + (1, 1)
+VECTOR_GROUPS = (15, 16)
 PROD_BUFS = 6
 PIECE = 256
 FIRST_PIECE_SLOT = 3
@@ -210,10 +210,12 @@ def tile_attention_pa_kernel(tc, hidden_states, cos, sin, w_qkv, out_0, out_1, o
             copy_x(2)
             quant_x(1, 2)
 
+        with tc.manual_schedule(engines={mybir.EngineType.DVE, mybir.EngineType.Pool}):
             pieces = [(c, g, h) for c in CHUNK_ORDER for g in range(PASSES) for h in range(N_TILE // PIECE)]
             rope_jobs = [(c, m) for c in range(ROPE_CHUNKS) for m in range(TOK_TILES)]
             group_of = [(g, k) for g, size in enumerate(GROUP_SIZES) for k in range(size)]
             prod = None
+            waiting = []
             for b, (c, m) in enumerate(rope_jobs):
                 group, place = group_of[b]
                 size = GROUP_SIZES[group]
@@ -237,12 +239,22 @@ def tile_attention_pa_kernel(tc, hidden_states, cos, sin, w_qkv, out_0, out_1, o
                 if place == 0:
                     prod = prod_pool.tile([P, size, 2, HEADS_PER_BANK, 2, HALF], F32, name="prod")
                 rope_products(m, acc, prod[:, place, :, :, :, :])
+                for job in waiting:
+                    rope_sum_store(nc.vector, job[0], job[1], job[2], job[3])
+                waiting.clear()
                 if b == 0:
                     quant_x(2, 4)
+                if b == 1:
+                    quant_x(4, 6)
                 if b == 3:
-                    quant_x(4, 8)
+                    quant_x(6, 8)
                 for qc in CHUNK_ORDER:
                     if QW_SLOT[qc] == b:
                         quant_w(qc)
                 if place == size - 1:
-                    rope_sum_store(nc.vector if group in VECTOR_GROUPS else nc.gpsimd, c, m - place, size, prod)
+                    if group not in VECTOR_GROUPS:
+                        rope_sum_store(nc.gpsimd, c, m - place, size, prod)
+                    elif b == len(rope_jobs) - 1:
+                        rope_sum_store(nc.vector, c, m - place, size, prod)
+                    else:
+                        waiting.append((c, m - place, size, prod))

@@ -27,13 +27,13 @@ ROPE_CHUNKS = 4
 N_CHUNKS = QKV // N_TILE
 
 LOAD_ORDER = (
-    ("x", 0), ("w", 0, 0), ("w", 0, 1), ("sin",), ("cos",), ("x", 1), ("x", 2), ("x", 3), ("x", 4), ("x", 5),
+    ("x", 0), ("w", 0, 0), ("w", 0, 1), ("x", 1), ("sin",), ("cos",), ("x", 2), ("x", 3), ("x", 4), ("x", 5),
     ("x", 6), ("x", 7), ("w", 1, 0), ("w", 1, 1), ("w", 4, 0), ("w", 4, 1), ("w", 2, 0), ("w", 2, 1),
 )
 LOAD_WIDTH = {0: N_TILE, 1: N_TILE, 2: 2 * N_TILE, 4: 2 * N_TILE}
 CHUNK_ORDER = (1, 4, 2, 5, 3)
 QW_SLOT = {1: 5, 4: 9, 2: 13, 5: 19, 3: 21}
-V_START = {4: 10, 5: 20}
+V_START = {4: 12, 5: 20}
 GROUP_SIZES = (2,) * 15 + (1, 1)
 VECTOR_GROUPS = (15, 16)
 PROD_BUFS = 6
@@ -74,8 +74,6 @@ def tile_attention_pa_kernel(tc, hidden_states, cos, sin, w_qkv, out_0, out_1, o
         sin_sb = keep.tile([P, TOK_TILES, DH], BF16, name="sin_sb")
         cos_sb = keep.tile([P, TOK_TILES, DH], BF16, name="cos_sb")
         table = keep.tile([P, TOK_TILES, 4, HALF], BF16, name="table")
-        warm_in = keep.tile([P, 8], F32, name="warm_in")
-        warm_out = keep.tile([P, 8], F32, name="warm_out")
         w_grp = {}
         x_bank = {}
 
@@ -186,8 +184,6 @@ def tile_attention_pa_kernel(tc, hidden_states, cos, sin, w_qkv, out_0, out_1, o
             nc.sync.dma_start(out=out_rows(c, m), in_=vres[:])
 
         with tc.manual_schedule():
-            nc.vector.memset(warm_in[:], 0.0)
-            nc.scalar.mul(out=warm_out[:], in_=warm_in[:], mul=-1.0)
             for item in LOAD_ORDER:
                 load(item)
 
@@ -195,22 +191,20 @@ def tile_attention_pa_kernel(tc, hidden_states, cos, sin, w_qkv, out_0, out_1, o
             copy_x(0)
             interleave_w(nc.vector.tensor_copy, 0, 0, 0)
             interleave_w(nc.scalar.copy, 0, 0, 1)
+            quant_x(0, 1)
             interleave_w(nc.vector.tensor_copy, 0, 1, 0)
             interleave_w(nc.vector.tensor_copy, 0, 1, 1, 0, 2)
             interleave_w(nc.scalar.copy, 0, 1, 1, 2, 4)
-            quant_x(0, 1)
             quant_w_pass(0, 0)
             quant_w_pass(0, 1)
-            nc.scalar.copy(out=table[:, :, 1, :], in_=sin_sb[:, :, HALF:DH])
-            nc.scalar.mul(out=table[:, :, 2, :], in_=sin_sb[:, :, 0:HALF], mul=-1.0)
-            nc.scalar.copy(out=table[:, :, 0:4:3, :], in_=cos_sb[:].rearrange("p m (s i) -> p m s i", s=2))
+            nc.vector.tensor_copy(out=table[:, :, 1, :], in_=sin_sb[:, :, HALF:DH])
+            nc.vector.tensor_scalar_mul(out=table[:, :, 2, :], in0=sin_sb[:, :, 0:HALF], scalar1=-1.0)
+            nc.vector.tensor_copy(out=table[:, :, 0:4:3, :], in_=cos_sb[:].rearrange("p m (s i) -> p m s i", s=2))
             transpose_x(1)
-            transpose_x(2)
             copy_x(1)
-            copy_x(2)
             quant_x(1, 2)
 
-        with tc.manual_schedule(engines={mybir.EngineType.DVE, mybir.EngineType.Pool}):
+        with tc.manual_schedule(engines={mybir.EngineType.DVE, mybir.EngineType.Pool, mybir.EngineType.Activation}):
             pieces = [(c, g, h) for c in CHUNK_ORDER for g in range(PASSES) for h in range(N_TILE // PIECE)]
             rope_jobs = [(c, m) for c in range(ROPE_CHUNKS) for m in range(TOK_TILES)]
             group_of = [(g, k) for g, size in enumerate(GROUP_SIZES) for k in range(size)]
@@ -226,8 +220,10 @@ def tile_attention_pa_kernel(tc, hidden_states, cos, sin, w_qkv, out_0, out_1, o
                         copy_x(t)
                 acc = matmul_bank(rope_ps, "rope_bank", c, m)
                 if b == 0:
-                    transpose_x(3)
-                    copy_x(3)
+                    for t in (2, 3):
+                        transpose_x(t)
+                    for t in (2, 3):
+                        copy_x(t)
                 for i, (pc, pg, ph) in enumerate(pieces):
                     if FIRST_PIECE_SLOT + (3 * i) // 4 == b:
                         interleave_w(nc.scalar.copy, pc, pg, ph)

@@ -27,7 +27,7 @@ ROPE_CHUNKS = 4
 N_CHUNKS = QKV // N_TILE
 
 LOAD_ORDER = (
-    ("x", 0), ("w", 0, 0), ("w", 0, 1), ("x", 1), ("sin",), ("cos",), ("x", 2), ("x", 3), ("x", 4), ("x", 5),
+    ("x", 0), ("w", 0, 0), ("w", 0, 1), ("x", 1), ("x", 2), ("sin",), ("cos",), ("x", 3), ("x", 4), ("x", 5),
     ("x", 6), ("x", 7), ("w", 1, 0), ("w", 1, 1), ("w", 4, 0), ("w", 4, 1), ("w", 2, 0), ("w", 2, 1),
 )
 LOAD_WIDTH = {0: N_TILE, 1: N_TILE, 2: 2 * N_TILE, 4: 2 * N_TILE}
@@ -39,6 +39,7 @@ VECTOR_GROUPS = (15, 16)
 PROD_BUFS = 6
 PIECE = 256
 FIRST_PIECE_SLOT = 3
+WARM_RUNS = (5, 4, 2)
 
 
 def tile_attention_pa_kernel(tc, hidden_states, cos, sin, w_qkv, out_0, out_1, out_2):
@@ -74,6 +75,8 @@ def tile_attention_pa_kernel(tc, hidden_states, cos, sin, w_qkv, out_0, out_1, o
         sin_sb = keep.tile([P, TOK_TILES, DH], BF16, name="sin_sb")
         cos_sb = keep.tile([P, TOK_TILES, DH], BF16, name="cos_sb")
         table = keep.tile([P, TOK_TILES, 4, HALF], BF16, name="table")
+        warm_l = keep.tile([P, P], BF16, name="warm_l")
+        warm_r = keep.tile([P, N_TILE], BF16, name="warm_r")
         w_grp = {}
         x_bank = {}
 
@@ -183,12 +186,21 @@ def tile_attention_pa_kernel(tc, hidden_states, cos, sin, w_qkv, out_0, out_1, o
             nc.scalar.copy(out=vres[:].rearrange("p h d -> p (h d)"), in_=acc[:])
             nc.sync.dma_start(out=out_rows(c, m), in_=vres[:])
 
+        def warm_up(bank, count):
+            for k in range(count):
+                nc.tensor.matmul(out=bank[:], lhsT=warm_l[:], rhs=warm_r[:], start=True, stop=True)
+
         with tc.manual_schedule():
+            nc.vector.memset(warm_l[:], 0.0)
+            nc.vector.memset(warm_r[:], 0.0)
             for item in LOAD_ORDER:
                 load(item)
 
+            warm_bank = rope_ps.tile([P, N_TILE], F32, name="rope_bank")
+            warm_up(warm_bank, WARM_RUNS[0])
             transpose_x(0)
             copy_x(0)
+            warm_up(warm_bank, WARM_RUNS[1])
             interleave_w(nc.vector.tensor_copy, 0, 0, 0)
             interleave_w(nc.scalar.copy, 0, 0, 1)
             quant_x(0, 1)
@@ -201,8 +213,12 @@ def tile_attention_pa_kernel(tc, hidden_states, cos, sin, w_qkv, out_0, out_1, o
             nc.vector.tensor_scalar_mul(out=table[:, :, 2, :], in0=sin_sb[:, :, 0:HALF], scalar1=-1.0)
             nc.vector.tensor_copy(out=table[:, :, 0:4:3, :], in_=cos_sb[:].rearrange("p m (s i) -> p m s i", s=2))
             transpose_x(1)
+            transpose_x(2)
+            warm_up(warm_bank, WARM_RUNS[2])
             copy_x(1)
+            copy_x(2)
             quant_x(1, 2)
+            early_banks = [matmul_bank(rope_ps, "rope_bank", 0, m) for m in range(2)]
 
         with tc.manual_schedule(engines={mybir.EngineType.DVE, mybir.EngineType.Pool, mybir.EngineType.Activation}):
             pieces = [(c, g, h) for c in CHUNK_ORDER for g in range(PASSES) for h in range(N_TILE // PIECE)]
@@ -218,12 +234,10 @@ def tile_attention_pa_kernel(tc, hidden_states, cos, sin, w_qkv, out_0, out_1, o
                         transpose_x(t)
                     for t in (2 * b + 2, 2 * b + 3):
                         copy_x(t)
-                acc = matmul_bank(rope_ps, "rope_bank", c, m)
+                acc = early_banks[b] if b < 2 else matmul_bank(rope_ps, "rope_bank", c, m)
                 if b == 0:
-                    for t in (2, 3):
-                        transpose_x(t)
-                    for t in (2, 3):
-                        copy_x(t)
+                    transpose_x(3)
+                    copy_x(3)
                 for i, (pc, pg, ph) in enumerate(pieces):
                     if FIRST_PIECE_SLOT + (3 * i) // 4 == b:
                         interleave_w(nc.scalar.copy, pc, pg, ph)

@@ -39,7 +39,7 @@ VECTOR_GROUPS = (15, 16)
 PROD_BUFS = 6
 PIECE = 256
 FIRST_PIECE_SLOT = 3
-WARM_RUNS = (5, 4, 2)
+WARM_RUNS = (5, 8, 3)
 
 
 def tile_attention_pa_kernel(tc, hidden_states, cos, sin, w_qkv, out_0, out_1, out_2):
@@ -253,11 +253,13 @@ def tile_attention_pa_kernel(tc, hidden_states, cos, sin, w_qkv, out_0, out_1, o
                     rope_sum_store(nc.vector, job[0], job[1], job[2], job[3])
                 waiting.clear()
                 if b == 0:
-                    quant_x(2, 4)
+                    quant_x(2, 3)
                 if b == 1:
-                    quant_x(4, 6)
+                    quant_x(3, 5)
                 if b == 3:
-                    quant_x(6, 8)
+                    quant_x(5, 7)
+                if b == 5:
+                    quant_x(7, 8)
                 for qc in CHUNK_ORDER:
                     if QW_SLOT[qc] == b:
                         quant_w(qc)

@@ -34,8 +34,9 @@ LOAD_WIDTH = {0: N_TILE, 1: N_TILE, 2: 2 * N_TILE, 4: 2 * N_TILE}
 CHUNK_ORDER = (1, 4, 2, 5, 3)
 QW_SLOT = {1: 5, 4: 9, 2: 13, 5: 19, 3: 21}
 V_START = {4: 12, 5: 20}
-GROUP_SIZES = (2,) * 15 + (1, 1)
-VECTOR_GROUPS = (15, 16)
+GROUP_SIZES = (2,) * 14 + (1, 1, 1, 1)
+TENSOR_GROUPS = (15,)
+VECTOR_GROUPS = (16, 17)
 PROD_BUFS = 6
 PIECE = 256
 FIRST_PIECE_SLOT = 3
@@ -186,6 +187,18 @@ def tile_attention_pa_kernel(tc, hidden_states, cos, sin, w_qkv, out_0, out_1, o
             nc.scalar.copy(out=vres[:].rearrange("p h d -> p (h d)"), in_=acc[:])
             nc.sync.dma_start(out=out_rows(c, m), in_=vres[:])
 
+        def rope_sum_on_tensor(c, m, prod):
+            total = aux_ps.tile([P, N_TILE], F32, name="aux_bank")
+            for run in range(2):
+                nc.tensor.matmul(
+                    out=total[:],
+                    lhsT=ident[:],
+                    rhs=prod[:, 0, run, :, :, :].rearrange("p h w i -> p (h w i)"),
+                    start=(run == 0),
+                    stop=(run == 1),
+                )
+            copy_v_store(c, m, total)
+
         def warm_up(bank, count):
             for k in range(count):
                 nc.tensor.matmul(out=bank[:], lhsT=warm_l[:], rhs=warm_r[:], start=True, stop=True)
@@ -264,7 +277,9 @@ def tile_attention_pa_kernel(tc, hidden_states, cos, sin, w_qkv, out_0, out_1, o
                     if QW_SLOT[qc] == b:
                         quant_w(qc)
                 if place == size - 1:
-                    if group not in VECTOR_GROUPS:
+                    if group in TENSOR_GROUPS:
+                        rope_sum_on_tensor(c, m, prod)
+                    elif group not in VECTOR_GROUPS:
                         rope_sum_store(nc.gpsimd, c, m - place, size, prod)
                     elif b == len(rope_jobs) - 1:
                         rope_sum_store(nc.vector, c, m - place, size, prod)

@@ -34,8 +34,8 @@ LOAD_WIDTH = {0: N_TILE, 1: N_TILE, 2: 2 * N_TILE, 4: 2 * N_TILE}
 CHUNK_ORDER = (1, 4, 2, 5, 3)
 QW_SLOT = {1: 5, 4: 9, 2: 13, 5: 19, 3: 21}
 V_START = {4: 12, 5: 20}
-GROUP_SIZES = (2,) * 14 + (1, 1, 1, 1)
-TENSOR_GROUPS = (15,)
+GROUP_SIZES = (2,) * 13 + (1, 1, 2, 1, 1)
+TENSOR_GROUPS = (14,)
 VECTOR_GROUPS = (16, 17)
 PROD_BUFS = 6
 PIECE = 256

@@ -33,12 +33,13 @@ LOAD_ORDER = (
 LOAD_WIDTH = {0: N_TILE, 1: N_TILE, 2: 2 * N_TILE, 4: 2 * N_TILE}
 CHUNK_ORDER = (1, 4, 2, 5, 3)
 QW_SLOT = {1: 5, 4: 9, 2: 13, 5: 19, 3: 21}
-V_START = {4: 12, 5: 20}
+V_START = {4: 14, 5: 20}
 GROUP_SIZES = (2,) * 13 + (1, 1, 2, 1, 1)
 TENSOR_GROUPS = (14,)
 VECTOR_GROUPS = (16, 17)
 PROD_BUFS = 6
 PIECE = 256
+SCALAR_RUN = 8
 FIRST_PIECE_SLOT = 3
 WARM_RUNS = (5, 8, 3)
 
@@ -119,15 +120,15 @@ def tile_attention_pa_kernel(tc, hidden_states, cos, sin, w_qkv, out_0, out_1, o
                 in_=x_grp[:, m0:m1, :, :, :].rearrange("p a g r t -> p (a g r t)"),
             )
 
-        def interleave_w(engine_copy, c, g, s, h0=0, h1=HEADS_PER_BANK):
+        def interleave_w(engine_copy, c, g, s, h0=0, h1=HEADS_PER_BANK, run=PACK):
             if c not in w_grp:
                 grouped = wgrp_pool.tile([P, PASSES, N_TILE, PACK], BF16, name="w_grouped", align_bytes=64)
                 w_grp[c] = grouped
             lo = s * PIECE + h0 * HALF
             hi = s * PIECE + h1 * HALF
             engine_copy(
-                out=w_grp[c][:, g, lo:hi, :].rearrange("p (u i) j -> p u j i", i=PACK),
-                in_=w_raw[(c, g)][:, :, lo:hi].rearrange("p j (u i) -> p u j i", i=PACK),
+                out=w_grp[c][:, g, lo:hi, :].rearrange("p (u i) j -> p u j i", i=run),
+                in_=w_raw[(c, g)][:, :, lo:hi].rearrange("p j (u i) -> p u j i", i=run),
             )
 
         def quant_w_pass(c, g):
@@ -253,7 +254,7 @@ def tile_attention_pa_kernel(tc, hidden_states, cos, sin, w_qkv, out_0, out_1, o
                     copy_x(3)
                 for i, (pc, pg, ph) in enumerate(pieces):
                     if FIRST_PIECE_SLOT + (3 * i) // 4 == b:
-                        interleave_w(nc.scalar.copy, pc, pg, ph)
+                        interleave_w(nc.scalar.copy, pc, pg, ph, run=SCALAR_RUN)
                 for vc in (4, 5):
                     vm = b - V_START[vc]
                     if 0 <= vm < TOK_TILES:

from contextlib import ExitStack

import concourse.mybir as mybir
from concourse.masks import make_identity

F32 = mybir.dt.float32
BF16 = mybir.dt.bfloat16
U32 = mybir.dt.uint32
U8 = mybir.dt.uint8
E5M2X4 = mybir.dt.float8_e5m2_x4
MULT = mybir.AluOpType.mult
ADD = mybir.AluOpType.add

SEQ, HID, HEADS, DH = 1024, 1024, 8, 128
QKV = 3 * HEADS * DH
FLOPS = 2 * SEQ * HID * QKV

P = 128
PACK = 4
K_PASS = P * PACK
PASSES = HID // K_PASS
N_TILE = 512
HEADS_PER_BANK = N_TILE // DH
HALF = DH // 2
TOK_TILES = SEQ // P
ROPE_CHUNKS = 4
N_CHUNKS = QKV // N_TILE

LOAD_ORDER = (
    ("x", 0), ("w", 0, 0), ("w", 0, 1), ("x", 1), ("x", 2), ("sin",), ("cos",), ("x", 3), ("x", 4), ("x", 5),
    ("x", 6), ("x", 7), ("w", 1, 0), ("w", 1, 1), ("w", 4, 0), ("w", 4, 1), ("w", 2, 0), ("w", 2, 1),
)
LOAD_WIDTH = {0: N_TILE, 1: N_TILE, 2: 2 * N_TILE, 4: 2 * N_TILE}
CHUNK_ORDER = (1, 4, 2, 5, 3)
QW_SLOT = {1: 5, 4: 9, 2: 13, 5: 19, 3: 21}
V_START = {4: 14, 5: 20}
GROUP_SIZES = (2,) * 13 + (1, 1, 2, 1, 1)
TENSOR_GROUPS = (14,)
VECTOR_GROUPS = (16, 17)
PROD_BUFS = 6
PIECE = 256
SCALAR_RUN = 8
FIRST_PIECE_SLOT = 3
WARM_RUNS = (5, 8, 3)


def tile_attention_pa_kernel(tc, hidden_states, cos, sin, w_qkv, out_0, out_1, out_2):
    nc = tc.nc
    x_rows = hidden_states[0, :, :].rearrange("(p m) k -> p m k", p=P)
    outs = [o[0, :, :, :].rearrange("(p m) h d -> p m h d", p=P) for o in (out_0, out_1, out_2)]

    with ExitStack() as ctx:
        keep = ctx.enter_context(tc.tile_pool(name="keep", bufs=1))
        wgrp_pool = ctx.enter_context(tc.tile_pool(name="wgrp_pool", bufs=3))
        prod_pool = ctx.enter_context(tc.tile_pool(name="prod_pool", bufs=PROD_BUFS))
        vres_pool = ctx.enter_context(tc.tile_pool(name="vres_pool", bufs=4))
        rope_ps = ctx.enter_context(tc.psum_pool(name="rope_ps", bufs=5))
        aux_ps = ctx.enter_context(tc.psum_pool(name="aux_ps", bufs=3))

        ident = keep.tile([P, P], F32, name="ident")
        make_identity(nc, ident[:])

        x_raw = [keep.tile([P, HID], BF16, name="x_raw%d" % m) for m in range(TOK_TILES)]
        x_grp = keep.tile([P, TOK_TILES, PASSES, P, PACK], BF16, name="x_grp", align_bytes=64)
        x_codes = keep.tile([P, TOK_TILES, PASSES * P], U32, name="x_codes", align_bytes=64)
        x_scales = keep.tile([P, TOK_TILES, PASSES * P], U8, name="x_scales", align_bytes=64)
        w_raw = {}
        for c in LOAD_WIDTH:
            width = LOAD_WIDTH[c]
            for g in range(PASSES):
                raw = keep.tile([P, PACK, width], BF16, name="w_raw%d_%d" % (c, g))
                for k in range(width // N_TILE):
                    w_raw[(c + k, g)] = raw[:, :, k * N_TILE:(k + 1) * N_TILE]
                w_raw[("load", c, g)] = raw
        w_codes = [keep.tile([P, PASSES, N_TILE], U32, name="w_codes%d" % c, align_bytes=64) for c in range(N_CHUNKS)]
        w_scales = [keep.tile([P, PASSES, N_TILE], U8, name="w_scales%d" % c, align_bytes=64) for c in range(N_CHUNKS)]
        sin_sb = keep.tile([P, TOK_TILES, DH], BF16, name="sin_sb")
        cos_sb = keep.tile([P, TOK_TILES, DH], BF16, name="cos_sb")
        table = keep.tile([P, TOK_TILES, 4, HALF], BF16, name="table")
        warm_l = keep.tile([P, P], BF16, name="warm_l")
        warm_r = keep.tile([P, N_TILE], BF16, name="warm_r")
        w_grp = {}
        x_bank = {}

        def load(item):
            if item[0] == "x":
                m = item[1]
                nc.sync.dma_start(out=x_raw[m][:], in_=x_rows[:, m, :])
            elif item[0] == "w":
                c, g = item[1], item[2]
                nc.sync.dma_start(
                    out=w_raw[("load", c, g)][:],
                    in_=w_qkv[g * K_PASS:(g + 1) * K_PASS, c * N_TILE:c * N_TILE + LOAD_WIDTH[c]].rearrange(
                        "(p j) w -> p j w", j=PACK),
                )
            elif item[0] == "sin":
                nc.sync.dma_start(out=sin_sb[:], in_=sin.rearrange("(p m) d -> p m d", p=P))
            else:
                nc.sync.dma_start(out=cos_sb[:], in_=cos.rearrange("(p m) d -> p m d", p=P))

        def transpose_x(m):
            bank = aux_ps.tile([P, N_TILE], F32, name="aux_bank")
            x_bank[m] = bank
            words = x_raw[m][:].bitcast(F32)
            view = bank[:].rearrange("p (g u r) -> p g u r", g=PASSES, u=2)
            for g in range(PASSES):
                for u in range(2):
                    nc.tensor.transpose(view[:, g, u, :], words[:, 256 * g + u:256 * (g + 1):2], ident[:])

        def copy_x(m):
            nc.scalar.copy(
                out=x_grp[:, m, :, :, :].bitcast(F32),
                in_=x_bank[m][:].rearrange("p (g u r) -> p g r u", g=PASSES, u=2),
            )

        def quant_x(m0, m1):
            nc.vector.quantize_mx(
                out=x_codes[:, m0:m1, :].rearrange("p a n -> p (a n)").bitcast(E5M2X4),
                scales=x_scales[:, m0:m1, :].rearrange("p a n -> p (a n)"),
                in_=x_grp[:, m0:m1, :, :, :].rearrange("p a g r t -> p (a g r t)"),
            )

        def interleave_w(engine_copy, c, g, s, h0=0, h1=HEADS_PER_BANK, run=PACK):
            if c not in w_grp:
                grouped = wgrp_pool.tile([P, PASSES, N_TILE, PACK], BF16, name="w_grouped", align_bytes=64)
                w_grp[c] = grouped
            lo = s * PIECE + h0 * HALF
            hi = s * PIECE + h1 * HALF
            engine_copy(
                out=w_grp[c][:, g, lo:hi, :].rearrange("p (u i) j -> p u j i", i=run),
                in_=w_raw[(c, g)][:, :, lo:hi].rearrange("p j (u i) -> p u j i", i=run),
            )

        def quant_w_pass(c, g):
            nc.vector.quantize_mx(
                out=w_codes[c][:, g, :].bitcast(E5M2X4),
                scales=w_scales[c][:, g, :],
                in_=w_grp[c][:, g, :, :].rearrange("p w j -> p (w j)"),
            )

        def quant_w(c):
            nc.vector.quantize_mx(
                out=w_codes[c][:].rearrange("p g w -> p (g w)").bitcast(E5M2X4),
                scales=w_scales[c][:].rearrange("p g w -> p (g w)"),
                in_=w_grp[c][:].rearrange("p g w j -> p (g w j)"),
            )

        def matmul_bank(pool, bank_name, c, m):
            acc = pool.tile([P, N_TILE], F32, name=bank_name)
            for g in range(PASSES):
                cols = slice(g * P, (g + 1) * P)
                nc.tensor.matmul_mx(
                    out=acc[:],
                    lhsT=x_codes[:, m, cols].bitcast(E5M2X4),
                    lhsT_scale=x_scales[:, m, cols],
                    rhs=w_codes[c][:, g, :].bitcast(E5M2X4),
                    rhs_scale=w_scales[c][:, g, :],
                    start=(g == 0),
                    stop=(g == PASSES - 1),
                )
            return acc

        def out_rows(c, m):
            h0 = (c % 2) * HEADS_PER_BANK
            return outs[c // 2][:, m, h0:h0 + HEADS_PER_BANK, :]

        def rope_products(m, acc, prod_bank):
            shape = [P, HEADS_PER_BANK, 2, 2, HALF]
            nc.vector.tensor_tensor(
                out=prod_bank.rearrange("p s h w i -> p h s w i"),
                in0=acc[:].rearrange("p (h s i) -> p h s i", s=2, i=HALF).unsqueeze(3).to_broadcast(shape),
                in1=table[:, m, :, :].rearrange("p (s w) i -> p s w i", s=2).unsqueeze(1).to_broadcast(shape),
                op=MULT,
            )

        def rope_sum_store(engine, c, m, size, prod):
            first = prod[:, :, 0, :, :, :].rearrange("p b h w i -> p b (h w i)")
            second = prod[:, :, 1, :, :, :].rearrange("p b h w i -> p b (h w i)")
            engine.tensor_tensor(out=first, in0=first, in1=second, op=ADD)
            h0 = (c % 2) * HEADS_PER_BANK
            nc.sync.dma_start(
                out=outs[c // 2][:, m:m + size, h0:h0 + HEADS_PER_BANK, :],
                in_=prod[:, :, 0, :, :, :].rearrange("p b h w i -> p b h (w i)"),
            )

        def copy_v_store(c, m, acc):
            vres = vres_pool.tile([P, HEADS_PER_BANK, DH], F32, name="vres")
            nc.scalar.copy(out=vres[:].rearrange("p h d -> p (h d)"), in_=acc[:])
            nc.sync.dma_start(out=out_rows(c, m), in_=vres[:])

        def rope_sum_on_tensor(c, m, prod):
            total = aux_ps.tile([P, N_TILE], F32, name="aux_bank")
            for run in range(2):
                nc.tensor.matmul(
                    out=total[:],
                    lhsT=ident[:],
                    rhs=prod[:, 0, run, :, :, :].rearrange("p h w i -> p (h w i)"),
                    start=(run == 0),
                    stop=(run == 1),
                )
            copy_v_store(c, m, total)

        def warm_up(bank, count):
            for k in range(count):
                nc.tensor.matmul(out=bank[:], lhsT=warm_l[:], rhs=warm_r[:], start=True, stop=True)

        with tc.manual_schedule():
            nc.vector.memset(warm_l[:], 0.0)
            nc.vector.memset(warm_r[:], 0.0)
            for item in LOAD_ORDER:
                load(item)

            warm_bank = rope_ps.tile([P, N_TILE], F32, name="rope_bank")
            warm_up(warm_bank, WARM_RUNS[0])
            transpose_x(0)
            copy_x(0)
            warm_up(warm_bank, WARM_RUNS[1])
            interleave_w(nc.vector.tensor_copy, 0, 0, 0)
            interleave_w(nc.scalar.copy, 0, 0, 1)
            quant_x(0, 1)
            interleave_w(nc.vector.tensor_copy, 0, 1, 0)
            interleave_w(nc.vector.tensor_copy, 0, 1, 1, 0, 2)
            interleave_w(nc.scalar.copy, 0, 1, 1, 2, 4)
            quant_w_pass(0, 0)
            quant_w_pass(0, 1)
            nc.vector.tensor_copy(out=table[:, :, 1, :], in_=sin_sb[:, :, HALF:DH])
            nc.vector.tensor_scalar_mul(out=table[:, :, 2, :], in0=sin_sb[:, :, 0:HALF], scalar1=-1.0)
            nc.vector.tensor_copy(out=table[:, :, 0:4:3, :], in_=cos_sb[:].rearrange("p m (s i) -> p m s i", s=2))
            transpose_x(1)
            transpose_x(2)
            warm_up(warm_bank, WARM_RUNS[2])
            copy_x(1)
            copy_x(2)
            quant_x(1, 2)
            early_banks = [matmul_bank(rope_ps, "rope_bank", 0, m) for m in range(2)]

        with tc.manual_schedule(engines={mybir.EngineType.DVE, mybir.EngineType.Pool, mybir.EngineType.Activation}):
            pieces = [(c, g, h) for c in CHUNK_ORDER for g in range(PASSES) for h in range(N_TILE // PIECE)]
            rope_jobs = [(c, m) for c in range(ROPE_CHUNKS) for m in range(TOK_TILES)]
            group_of = [(g, k) for g, size in enumerate(GROUP_SIZES) for k in range(size)]
            prod = None
            waiting = []
            for b, (c, m) in enumerate(rope_jobs):
                group, place = group_of[b]
                size = GROUP_SIZES[group]
                if b in (1, 2):
                    for t in (2 * b + 2, 2 * b + 3):
                        transpose_x(t)
                    for t in (2 * b + 2, 2 * b + 3):
                        copy_x(t)
                acc = early_banks[b] if b < 2 else matmul_bank(rope_ps, "rope_bank", c, m)
                if b == 0:
                    transpose_x(3)
                    copy_x(3)
                for i, (pc, pg, ph) in enumerate(pieces):
                    if FIRST_PIECE_SLOT + (3 * i) // 4 == b:
                        interleave_w(nc.scalar.copy, pc, pg, ph, run=SCALAR_RUN)
                for vc in (4, 5):
                    vm = b - V_START[vc]
                    if 0 <= vm < TOK_TILES:
                        vacc = matmul_bank(aux_ps, "aux_bank", vc, vm)
                        copy_v_store(vc, vm, vacc)
                if place == 0:
                    prod = prod_pool.tile([P, size, 2, HEADS_PER_BANK, 2, HALF], F32, name="prod")
                rope_products(m, acc, prod[:, place, :, :, :, :])
                for job in waiting:
                    rope_sum_store(nc.vector, job[0], job[1], job[2], job[3])
                waiting.clear()
                if b == 0:
                    quant_x(2, 3)
                if b == 1:
                    quant_x(3, 5)
                if b == 3:
                    quant_x(5, 7)
                if b == 5:
                    quant_x(7, 8)
                for qc in CHUNK_ORDER:
                    if QW_SLOT[qc] == b:
                        quant_w(qc)
                if place == size - 1:
                    if group in TENSOR_GROUPS:
                        rope_sum_on_tensor(c, m, prod)
                    elif group not in VECTOR_GROUPS:
                        rope_sum_store(nc.gpsimd, c, m - place, size, prod)
                    elif b == len(rope_jobs) - 1:
                        rope_sum_store(nc.vector, c, m - place, size, prod)
                    else:
                        waiting.append((c, m - place, size, prod))
